import numpy as np
import ml_dtypes


BF16 = ml_dtypes.bfloat16


def bf(x):
    return np.asarray(x, np.float32).astype(BF16)


def f64(x):
    return np.asarray(x).astype(np.float64)


E2M1 = np.array([0.0, 0.5, 1.0, 1.5, 2.0, 3.0, 4.0, 6.0, -0.0, -0.5, -1.0, -1.5, -2.0, -3.0, -4.0, -6.0])


def pack_weight(w, fmt):
    k, n = w.shape
    w = f64(bf(w)).reshape(k // 32, 32, n)
    amax = np.abs(w).max(1)
    if fmt == "e4m3":
        byte = np.frexp(amax)[1] - 1 + 127 - 7
    else:
        mant, ex = np.frexp(amax / 6.0)
        byte = np.where(mant > 0.5, ex, ex - 1) + 127
    byte = np.clip(np.where(amax > 0, byte, 1), 1, 254)
    scaled = (w * np.exp2(127.0 - byte)[:, None, :]).reshape(k, n).astype(np.float32)
    by_word = np.ascontiguousarray(scaled.reshape(k // 512, 128, 4, n).transpose(0, 1, 3, 2))
    if fmt == "e4m3":
        words = by_word.astype(ml_dtypes.float8_e4m3fn).view(np.uint8)
    else:
        c = by_word.astype(ml_dtypes.float4_e2m1fn).view(np.uint8) & 0xF
        words = c[..., 0::2] | (c[..., 1::2] << 4)
    return np.ascontiguousarray(words), np.ascontiguousarray(byte.astype(np.uint8).reshape(k // 512, 16, n))


def unpack_weight(words, scales, fmt):
    g, p, n, _ = words.shape
    if fmt == "e4m3":
        vals = np.ascontiguousarray(words).view(ml_dtypes.float8_e4m3fn).astype(np.float64)
    else:
        nib = np.empty((g, p, n, 4), np.uint8)
        nib[..., 0::2] = words & 0xF
        nib[..., 1::2] = words >> 4
        vals = E2M1[nib]
    vals = vals * np.repeat(np.exp2(scales.astype(np.float64) - 127.0), 8, axis=1)[..., None]
    return vals.transpose(0, 1, 3, 2).reshape(g * 512, n)

def pack4(w):
    words, scales = pack_weight(w, "e2m1")
    return words.reshape(words.shape[0], 128, -1), scales


def unpack4(words, scales):
    return unpack_weight(words.reshape(words.shape[0], 128, -1, 2), scales, "e2m1")


def kspread(k):
    return np.exp2(np.repeat(np.random.randint(-6, 7, k // 32), 32).astype(np.float64))


B, S, HID, H, HK, D = 2, 128, 8192, 16, 4, 128
EPS = 1e-6
PRE = 0.004


def rmsnorm(v, w):
    var = np.mean(v * v, axis=-1, keepdims=True)
    return w * (v * (1.0 / np.sqrt(var + EPS)))


def rope(v, cos, sin):
    c = cos[:, :, None, :]
    sn = sin[:, :, None, :]
    v1, v2 = np.split(v, 2, axis=-1)
    rot = np.concatenate([-v2, v1], axis=-1)
    return v * c + rot * sn


def setup_inputs():
    s = kspread(HID)
    hidden_states = np.random.standard_normal((B, S, HID)) * s
    cos = bf(np.cos(np.random.standard_normal((B, S, D))))
    sin = bf(np.sin(np.random.standard_normal((B, S, D))))
    wq = np.random.standard_normal((H * D, HID)) * PRE / np.sqrt(HID) / s
    wk = np.random.standard_normal((HK * D, HID)) * PRE / np.sqrt(HID) / s
    q_norm_w = bf(1.0 + 0.1 * np.random.standard_normal(D))
    k_norm_w = bf(1.0 + 0.1 * np.random.standard_normal(D))
    hidden_states_words, hidden_states_scales = pack4(np.ascontiguousarray(hidden_states.reshape(B * S, HID).T))
    wq_words, wq_scales = pack4(np.ascontiguousarray(wq.T))
    wk_words, wk_scales = pack4(np.ascontiguousarray(wk.T))
    return {
        "hidden_states_words": hidden_states_words,
        "hidden_states_scales": hidden_states_scales,
        "cos": cos,
        "sin": sin,
        "Wq_query_words": wq_words,
        "Wq_query_scales": wq_scales,
        "Wk_words": wk_words,
        "Wk_scales": wk_scales,
        "q_norm_w": q_norm_w,
        "k_norm_w": k_norm_w,
    }


def reference(hidden_states_words, hidden_states_scales, cos, sin, Wq_query_words, Wq_query_scales, Wk_words, Wk_scales, q_norm_w, k_norm_w):
    xq = unpack4(hidden_states_words, hidden_states_scales).T.reshape(B, S, HID)
    q = (xq @ unpack4(Wq_query_words, Wq_query_scales)).reshape(B, S, H, D)
    k = (xq @ unpack4(Wk_words, Wk_scales)).reshape(B, S, HK, D)
    q = rmsnorm(q, f64(q_norm_w))
    k = rmsnorm(k, f64(k_norm_w))
    q = rope(q, f64(cos), f64(sin))
    k = rope(k, f64(cos), f64(sin))
    return q, k

from contextlib import ExitStack

import concourse.mybir as mybir

F32 = mybir.dt.float32
BF16 = mybir.dt.bfloat16
U8 = mybir.dt.uint8
I32 = mybir.dt.int32
FP4X4 = mybir.dt.float4_e2m1fn_x4
ALU = mybir.AluOpType
ACT = mybir.ActivationFunctionType

P = 128
PASSES = 16
TOKEN_TILES = 2
HEAD = 128
HALF = HEAD // 2
BANK = 512
EPS = 1e-6

FLOPS = 2 * 256 * 8192 * 2560

WARM_UP_MATMULS = 11
FINISH_FROM = 10


def split_runs(lengths):
    runs = []
    first = 0
    for n in lengths:
        runs.append((first, first + n))
        first += n
    return runs


def tile_qwen3nextattentionforengine_pa_kernel(
    tc,
    hidden_states_words,
    hidden_states_scales,
    cos,
    sin,
    Wq_query_words,
    Wq_query_scales,
    Wk_words,
    Wk_scales,
    q_norm_w,
    k_norm_w,
    out_0,
    out_1,
):
    nc = tc.nc

    with ExitStack() as ctx:
        keep = ctx.enter_context(tc.tile_pool(name="keep", bufs=1))
        work = ctx.enter_context(tc.tile_pool(name="work", bufs=3))
        stat = ctx.enter_context(tc.tile_pool(name="stat", bufs=6))
        psum = ctx.enter_context(tc.psum_pool(name="psum", bufs=1))
        ctx.enter_context(tc.manual_schedule())

        def operand(label, words, scales, first_col, cols, code_lengths, scale_lengths):
            op = {
                "words": words,
                "scales": scales,
                "first_col": first_col,
                "cols": cols,
                "code_runs": split_runs(code_lengths),
                "scale_runs": split_runs(scale_lengths),
                "codes": {},
                "planes": {},
            }
            for g0, g1 in op["code_runs"]:
                t = keep.tile([P, g1 - g0, 2 * cols], U8, name="%s_codes_%d" % (label, g0), align_bytes=64)
                for g in range(g0, g1):
                    op["codes"][g] = (t, g - g0)
            for g0, g1 in op["scale_runs"]:
                t = keep.tile([P, g1 - g0, cols], U8, name="%s_plane_%d" % (label, g0), align_bytes=64)
                for g in range(g0, g1):
                    op["planes"][g] = (t, g - g0)
            return op

        x_op = operand("x", hidden_states_words, hidden_states_scales, 0, 256, [2, 2, 4, 4, 4], [16])
        a_op = operand("a", Wq_query_words, Wq_query_scales, 0, 1536, [1] * 16, [2] * 8)
        b_op = operand("b", Wq_query_words, Wq_query_scales, 1536, 512, [2, 2, 4, 4, 4], [8, 8])
        k_op = operand("k", Wk_words, Wk_scales, 0, 512, [4, 4, 4, 4], [8, 8])

        loads = []
        for ops in ([x_op, a_op], [b_op], [k_op]):
            for g in range(PASSES):
                code_loads = [("codes", op, run) for op in ops for run in op["code_runs"] if run[0] == g]
                scale_loads = [("scales", op, run) for op in ops for run in op["scale_runs"] if run[0] == g]
                if len(loads) == 0:
                    loads.append(code_loads[0])
                    loads.append(("codes", a_op, (0, 1, (0, 2 * BANK))))
                    loads.extend(scale_loads)
                    loads.append(("codes", a_op, (0, 1, (2 * BANK, 6 * BANK))))
                else:
                    loads.extend(scale_loads + code_loads)
                if ops[0] is x_op and g == 6:
                    loads.append(("tables", x_op, (0, 0)))

        ones = keep.tile([P, P], BF16, name="ones")
        nc.gpsimd.memset(ones[:], 1.0)
        zeros = keep.tile([P, BANK], BF16, name="zeros")
        nc.gpsimd.memset(zeros[:], 0.0)
        seed = keep.tile([P, 1], F32, name="seed")
        nc.gpsimd.memset(seed[:], 1.0)
        seed_root = keep.tile([P, 1], F32, name="seed_root")
        nc.scalar.activation(out=seed_root[:], in_=seed[:], func=ACT.Abs_reciprocal_sqrt)
        gain_rows = keep.tile([P, 2 * HEAD], BF16, name="gain_rows")
        nc.gpsimd.memset(gain_rows[:], 0.0)
        cos_sb = keep.tile([P, TOKEN_TILES, HEAD], BF16, name="cos_sb")
        sin_sb = keep.tile([P, TOKEN_TILES, HEAD], BF16, name="sin_sb")

        for kind, op, run in loads:
            if kind == "scales":
                plane = op["planes"][run[0]][0]
                nc.vector.memset(plane[:].bitcast(I32), 0)

        for kind, op, run in loads:
            g0, g1 = run[0], run[1]
            c0 = op["first_col"]
            c1 = c0 + op["cols"]
            if kind == "codes":
                t = op["codes"][g0][0]
                b0, b1 = run[2] if len(run) == 3 else (0, 2 * op["cols"])
                nc.sync.dma_start(
                    out=t[:, :, b0:b1].bitcast(I32),
                    in_=op["words"][g0:g1, :, 2 * c0 + b0 : 2 * c0 + b1].rearrange("g p b -> p g b").bitcast(I32),
                )
            elif kind == "tables":
                nc.sync.dma_start(out=gain_rows[0:1, 0:HEAD], in_=q_norm_w.rearrange("(o d) -> o d", o=1))
                nc.sync.dma_start(out=gain_rows[0:1, HEAD : 2 * HEAD], in_=k_norm_w.rearrange("(o d) -> o d", o=1))
                nc.sync.dma_start(out=cos_sb[:], in_=cos.rearrange("b s d -> s b d"))
                nc.sync.dma_start(out=sin_sb[:], in_=sin.rearrange("b s d -> s b d"))
            else:
                t = op["planes"][g0][0]
                for r in range(4):
                    nc.sync.dma_start(
                        out=t[r:P:32, :, :].bitcast(I32),
                        in_=op["scales"][g0:g1, r:16:4, c0:c1].rearrange("g q c -> q g c").bitcast(I32),
                    )


        def bank(i, cols):
            return psum.tile([P, cols], F32, name="bank%d" % i, tag="bank%d" % i)

        def mx_pass(acc, op, g, tt, col, n):
            xc, xi = x_op["codes"][g]
            xp, xj = x_op["planes"][g]
            wc, wi = op["codes"][g]
            wp, wj = op["planes"][g]
            nc.tensor.matmul_mx(
                out=acc[:, 0:n],
                lhsT=xc[:, xi, 2 * P * tt : 2 * P * (tt + 1)].bitcast(FP4X4),
                lhsT_scale=xp[:, xj, P * tt : P * (tt + 1)],
                rhs=wc[:, wi, 2 * col : 2 * (col + n)].bitcast(FP4X4),
                rhs_scale=wp[:, wj, col : col + n],
                start=(g == 0),
                stop=(g == PASSES - 1),
            )

        scratch = bank(7, BANK)
        for i in range(WARM_UP_MATMULS):
            nc.tensor.matmul(out=scratch[:], lhsT=ones[:], rhs=zeros[:], start=True, stop=True)

        gains = bank(6, BANK)
        a_acc = [[bank(3 * tt + cb, BANK) for cb in range(3)] for tt in range(TOKEN_TILES)]
        for g in range(PASSES):
            for cb in range(3):
                for tt in range(TOKEN_TILES):
                    mx_pass(a_acc[tt][cb], a_op, g, tt, BANK * cb, BANK)
            if g == 9:
                nc.tensor.matmul(out=gains[:, 0 : 2 * HEAD], lhsT=ones[:], rhs=gain_rows[:], start=True, stop=True)

        tables = []
        for kind in range(2):
            k0 = kind * HEAD
            row = []
            for tt in range(TOKEN_TILES):
                tab = keep.tile([P, 2, HEAD], F32, name="table_%d_%d" % (kind, tt))
                nc.vector.tensor_tensor(out=tab[:, 0, :], in0=gains[:, k0 : k0 + HEAD], in1=cos_sb[:, tt, :], op=ALU.mult)
                nc.vector.tensor_tensor(
                    out=tab[:, 1, 0:HALF], in0=gains[:, k0 : k0 + HALF], in1=sin_sb[:, tt, HALF:HEAD], op=ALU.mult
                )
                nc.vector.scalar_tensor_tensor(
                    out=tab[:, 1, HALF:HEAD],
                    in0=gains[:, k0 + HALF : k0 + HEAD],
                    scalar=-1.0,
                    in1=sin_sb[:, tt, 0:HALF],
                    op0=ALU.mult,
                    op1=ALU.mult,
                )
                row.append(tab)
            tables.append(row)

        b_acc = [bank(6 + tt, BANK) for tt in range(TOKEN_TILES)]
        for g in range(PASSES):
            for tt in range(TOKEN_TILES):
                mx_pass(b_acc[tt], b_op, g, tt, 0, BANK)

        q_out = [keep.tile([P, 16 * HEAD], F32, name="q_out_%d" % tt) for tt in range(TOKEN_TILES)]
        k_out = [keep.tile([P, 4 * HEAD], F32, name="k_out_%d" % tt) for tt in range(TOKEN_TILES)]

        def mean_squares(job):
            heads = job["heads"]
            sums = stat.tile([P, heads], F32, name="sums", tag="sums%d" % heads)
            for h in range(heads):
                squares = work.tile([P, HEAD], F32, name="squares")
                nc.scalar.activation(
                    out=squares[:],
                    in_=job["acc"][:, h * HEAD : (h + 1) * HEAD],
                    func=ACT.Square,
                    accum_out=sums[:, h : h + 1],
                )
            rstd = stat.tile([P, heads], F32, name="rstd", tag="rstd%d" % heads)
            nc.scalar.activation(out=rstd[:], in_=sums[:], func=ACT.Abs_reciprocal_sqrt, scale=1.0 / HEAD, bias=EPS)
            job["rstd"] = rstd

        def products(job):
            heads = job["heads"]
            prod = work.tile([P, 2, heads, HEAD], F32, name="prod", tag="prod%d" % heads)
            v = job["acc"][:, 0 : heads * HEAD].rearrange("p (h d) -> p h d", h=heads)
            for r in range(2):
                nc.vector.tensor_tensor(
                    out=prod[:, r, :, :],
                    in0=v,
                    in1=job["table"][:, r : r + 1, :].to_broadcast([P, heads, HEAD]),
                    op=ALU.mult,
                )
            job["prod"] = prod

        def combine(job, engine):
            prod = job["prod"]
            dest = job["dest"]
            engine.tensor_tensor(out=dest[:, :, 0:HALF], in0=prod[:, 0, :, 0:HALF], in1=prod[:, 1, :, HALF:HEAD], op=ALU.add)
            engine.tensor_tensor(out=dest[:, :, HALF:HEAD], in0=prod[:, 0, :, HALF:HEAD], in1=prod[:, 1, :, 0:HALF], op=ALU.add)

        def scale(job):
            dest = job["dest"]
            for h in range(job["heads"]):
                nc.scalar.activation(out=dest[:, h, :], in_=dest[:, h, :], func=ACT.Copy, scale=job["rstd"][:, h : h + 1])

        def q_job(acc, tt, cb):
            return {
                "acc": acc,
                "heads": 4,
                "table": tables[0][tt],
                "dest": q_out[tt][:, BANK * cb : BANK * (cb + 1)].rearrange("p (h d) -> p h d", h=4),
            }

        jobs = [q_job(a_acc[tt][cb], tt, cb) for cb in range(3) for tt in range(TOKEN_TILES)]
        jobs.extend([q_job(b_acc[tt], tt, 3) for tt in range(TOKEN_TILES)])
        for i in range(len(jobs) + 2):
            if i < len(jobs):
                mean_squares(jobs[i])
                products(jobs[i])
                combine(jobs[i], nc.gpsimd)
            if i >= 2:
                scale(jobs[i - 2])
                done = i - 2
                if done == 4 or done == 5:
                    tt = done - 4
                    nc.sync.dma_start(
                        out=out_0[tt, :, 0:12, :].rearrange("s h d -> s (h d)"), in_=q_out[tt][:, 0 : 3 * BANK]
                    )
                if done >= 6:
                    tt = done - 6
                    nc.sync.dma_start(
                        out=out_0[tt, :, 12:16, :].rearrange("s h d -> s (h d)"), in_=q_out[tt][:, 3 * BANK : 4 * BANK]
                    )

        groups = [(tt, half) for tt in range(TOKEN_TILES) for half in range(2)]
        k_acc = [bank(i, BANK // 2) for i in range(len(groups))]
        for g in range(FINISH_FROM):
            for i, (tt, half) in enumerate(groups):
                mx_pass(k_acc[i], k_op, g, tt, 256 * half, 256)
        for i, (tt, half) in enumerate(groups):
            for g in range(FINISH_FROM, PASSES):
                mx_pass(k_acc[i], k_op, g, tt, 256 * half, 256)

        k_jobs = [
            {
                "acc": k_acc[i],
                "heads": 2,
                "table": tables[1][tt],
                "dest": k_out[tt][:, 256 * half : 256 * (half + 1)].rearrange("p (h d) -> p h d", h=2),
            }
            for i, (tt, half) in enumerate(groups)
        ]
        for i in range(len(k_jobs) + 1):
            if i < len(k_jobs):
                products(k_jobs[i])
                mean_squares(k_jobs[i])
                combine(k_jobs[i], nc.vector if i == len(k_jobs) - 1 else nc.gpsimd)
            if i >= 1:
                scale(k_jobs[i - 1])
                tt, half = groups[i - 1]
                nc.sync.dma_start(
                    out=out_1[tt, :, 2 * half : 2 * half + 2, :].rearrange("s h d -> s (h d)"),
                    in_=k_out[tt][:, 256 * half : 256 * (half + 1)],
                )
